import numpy as np
import ml_dtypes


def mxq(x, axis, fmt="e4m3"):
    dtype, down = {"e4m3": (ml_dtypes.float8_e4m3fn, 7), "e5m2": (ml_dtypes.float8_e5m2, 14)}[fmt]
    v = np.moveaxis(np.asarray(x, np.float32).astype(ml_dtypes.bfloat16).astype(np.float64), axis, -1)
    blocks = v.reshape(v.shape[:-1] + (-1, 32))
    amax = np.abs(blocks).max(-1, keepdims=True)
    byte = np.maximum(np.where(amax > 0, np.frexp(amax)[1] - 1 + 127, 0) - down, 1)
    scale = np.exp2(byte - 127.0)
    codes = (blocks / scale).astype(np.float32).astype(dtype).astype(np.float64)
    return np.moveaxis((codes * scale).reshape(v.shape), -1, axis)


WIDE = False


def mx_kscale(k):
    if not WIDE:
        return np.ones(k)
    levels = np.array([10, -10, 5, -5, 0])
    if k % 512:
        return np.exp2(np.random.permutation(np.resize(levels, k // 32))).repeat(32)
    a = np.empty((k // 512, 16))
    for p in range(k // 512):
        a[p, :8] = np.random.permutation(np.resize(levels, 8))
        for g in range(8):
            far = levels[np.abs(levels - a[p, g]) >= 10]
            a[p, g + 8] = far[np.random.randint(len(far))]
    return np.exp2(a.ravel()).repeat(32)


BF16 = ml_dtypes.bfloat16


def bf(x):
    return np.asarray(x, np.float32).astype(BF16)


def f64(x):
    return np.asarray(x).astype(np.float64)


B, T, DM, DH, L = 4, 2048, 512, 256, 512


def setup_inputs():
    s, u = mx_kscale(DM), mx_kscale(DM)
    return {"k": bf(np.random.standard_normal((B, T, DM)) * s),
            "v": bf(np.random.standard_normal((B, T, DM)) * u),
            "Wk": bf(np.random.standard_normal((DH, DM)) / np.sqrt(DM) / s),
            "Wv": bf(np.random.standard_normal((DH, DM)) * 3.0 / np.sqrt(DM) / u)}


def reference(k, v, Wk, Wv):
    K = mxq(f64(k), 2, "e4m3") @ mxq(f64(Wk), 1, "e4m3").T
    V = mxq(f64(v), 2, "e4m3") @ mxq(f64(Wv), 1, "e4m3").T
    max_key = K.max(axis=0, keepdims=True)
    exp_key = np.exp(K - max_key)
    return exp_key * V, exp_key

@@ -1,0 +1,193 @@
+from contextlib import ExitStack
+
+import concourse.mybir as mybir
+from concourse.masks import make_identity
+
+F32 = mybir.dt.float32
+BF16 = mybir.dt.bfloat16
+U32 = mybir.dt.uint32
+U8 = mybir.dt.uint8
+FP8X4 = mybir.dt.float8_e4m3fn_x4
+
+P = 128
+PACK = 4
+B, T, DM, DH = 4, 2048, 512, 256
+WORDS = DM // 2
+HALVES = DH // P
+STEPS = T // P
+J_LOAD = 2
+J_STORE = 4
+LOAD_BUFS = 4
+STORE_BUFS = 3
+CHUNKS = STEPS // J_LOAD
+HEAD_CHUNKS = 2
+
+FLOPS = 2 * 2 * B * T * DM * DH
+
+
+def tile_aftfull_pa_t_kernel(tc, k, v, Wk, Wv, out_0, out_1):
+    nc = tc.nc
+    with ExitStack() as ctx:
+        consts = ctx.enter_context(tc.tile_pool(name="consts", bufs=1))
+        loads = ctx.enter_context(tc.tile_pool(name="loads", bufs=LOAD_BUFS))
+        stage = ctx.enter_context(tc.tile_pool(name="stage", bufs=2))
+        maxima = ctx.enter_context(tc.tile_pool(name="maxima", bufs=2 * HALVES))
+        results = ctx.enter_context(tc.tile_pool(name="results", bufs=STORE_BUFS))
+        psum_t = ctx.enter_context(tc.psum_pool(name="psum_t", bufs=4))
+        psum_k = ctx.enter_context(tc.psum_pool(name="psum_k", bufs=HALVES))
+        psum_v = ctx.enter_context(tc.psum_pool(name="psum_v", bufs=HALVES))
+        ctx.enter_context(tc.manual_schedule())
+
+        k_rows = k.rearrange("b (p j) d -> p b j d", j=STEPS)
+        v_rows = v.rearrange("b (p j) d -> p b j d", j=STEPS)
+        ev_rows = out_0.rearrange("b (p j) c -> p b j c", j=STEPS)
+        e_rows = out_1.rearrange("b (p j) c -> p b j c", j=STEPS)
+
+        k_chunks = {}
+        v_chunks = {}
+
+        def fetch(c):
+            k_chunk = loads.tile([P, B, J_LOAD, DM], BF16)
+            v_chunk = loads.tile([P, B, J_LOAD, DM], BF16)
+            piece = 1 if c < HEAD_CHUNKS else J_LOAD
+            for first in range(0, J_LOAD, piece):
+                inside = slice(first, first + piece)
+                steps = slice(c * J_LOAD + first, c * J_LOAD + first + piece)
+                nc.sync.dma_start(out=k_chunk[:, :, inside, :], in_=k_rows[:, :, steps, :])
+                nc.sync.dma_start(out=v_chunk[:, :, inside, :], in_=v_rows[:, :, steps, :])
+            k_chunks[c] = k_chunk
+            v_chunks[c] = v_chunk
+
+        def refill_after(g):
+            if g % J_LOAD == J_LOAD - 1 and g // J_LOAD + LOAD_BUFS < CHUNKS:
+                fetch(g // J_LOAD + LOAD_BUFS)
+
+        def store(rows, result, g):
+            jj = g % J_STORE
+            if g >= STEPS - J_STORE:
+                lo, hi = jj, jj + 1
+            elif jj == J_STORE - 1:
+                lo, hi = 0, J_STORE
+            else:
+                return
+            nc.sync.dma_start(out=rows[:, :, g - jj + lo : g - jj + hi, :], in_=result[:, :, lo:hi, :])
+
+        def rows_of_step(chunks, g):
+            words = chunks[g // J_LOAD][:].bitcast(F32)
+            return [words[:, b, g % J_LOAD, :] for b in range(B)]
+
+        def transpose_rows(rows):
+            banks = []
+            for pair in range(2):
+                xt = psum_t.tile([P, 2, 2, P], F32)
+                for i in range(2):
+                    for u in range(2):
+                        nc.tensor.transpose(xt[:, i, u, :], rows[2 * pair + i][:, u:WORDS:2], identity[:])
+                banks.append(xt)
+            return banks
+
+        def regroup(banks, which):
+            grouped = stage.tile([P, B, P, PACK], BF16, tag="grouped_" + which, align_bytes=64)
+            words = grouped[:].bitcast(F32)
+            for pair in range(2):
+                nc.scalar.copy(out=words[:, 2 * pair : 2 * pair + 2, :, :], in_=banks[pair][:].rearrange("p i u r -> p i r u"))
+            return grouped
+
+        def quantise(pool, grouped, which):
+            codes = pool.tile([P, B * P], U32, tag="codes_" + which, align_bytes=64)
+            scales = pool.tile([P, B * P], U8, tag="scales_" + which, align_bytes=64)
+            nc.vector.quantize_mx(
+                out=codes[:].bitcast(FP8X4), scales=scales[:], in_=grouped[:].rearrange("p b r t -> p (b r t)")
+            )
+            return codes, scales
+
+        def project(pool, operand, first_w_block):
+            codes, scales = operand
+            accs = []
+            for h in range(HALVES):
+                acc = pool.tile([P, B, P], F32)
+                w_cols = slice((first_w_block + h) * P, (first_w_block + h + 1) * P)
+                for b in range(B):
+                    tokens = slice(b * P, (b + 1) * P)
+                    nc.tensor.matmul_mx(
+                        out=acc[:, b, :],
+                        lhsT=codes[:, tokens].bitcast(FP8X4),
+                        lhsT_scale=scales[:, tokens],
+                        rhs=w_codes[:, w_cols].bitcast(FP8X4),
+                        rhs_scale=w_scales[:, w_cols],
+                        start=True,
+                        stop=True,
+                    )
+                accs.append(acc)
+            return accs
+
+        identity = consts.tile([P, P], F32)
+        make_identity(nc, identity[:])
+        warm = consts.tile([P, 1], F32)
+        nc.vector.memset(warm[:], 0.0)
+        nc.scalar.activation(out=warm[:], in_=warm[:], func=mybir.ActivationFunctionType.Exp)
+
+        w_raw = consts.tile([P, 2 * HALVES, DM], BF16)
+        nc.sync.dma_start(out=w_raw[:, 0:HALVES, :], in_=Wk.rearrange("(i p) d -> p i d", p=P))
+        nc.sync.dma_start(out=w_raw[:, HALVES : 2 * HALVES, :], in_=Wv.rearrange("(i p) d -> p i d", p=P))
+        for c in range(LOAD_BUFS):
+            fetch(c)
+
+        w_words = w_raw[:].bitcast(F32)
+        w_grouped = regroup(transpose_rows([w_words[:, i, :] for i in range(2 * HALVES)]), "w")
+        w_codes, w_scales = quantise(consts, w_grouped, "w")
+
+        k_grouped = {}
+        v_grouped = {}
+        k_grouped[0] = regroup(transpose_rows(rows_of_step(k_chunks, 0)), "k")
+        v_grouped[0] = regroup(transpose_rows(rows_of_step(v_chunks, 0)), "v")
+        k_acc = project(psum_k, quantise(stage, k_grouped[0], "k"), 0)
+        v_operand = quantise(stage, v_grouped[0], "v")
+        k_grouped[1] = regroup(transpose_rows(rows_of_step(k_chunks, 1)), "k")
+        v_grouped[1] = regroup(transpose_rows(rows_of_step(v_chunks, 1)), "v")
+        refill_after(0)
+        refill_after(1)
+
+        for g in range(STEPS):
+            ahead = g + 2
+            jj = g % J_STORE
+            if jj == 0:
+                e_tile = results.tile([P, B, J_STORE, DH], F32)
+                ev_tile = results.tile([P, B, J_STORE, DH], F32)
+
+            if ahead < STEPS:
+                k_grouped[ahead] = regroup(transpose_rows(rows_of_step(k_chunks, ahead)), "k")
+                v_banks = transpose_rows(rows_of_step(v_chunks, ahead))
+                refill_after(ahead)
+            v_acc = project(psum_v, v_operand, HALVES)
+
+            tops = []
+            for h in range(HALVES):
+                top = maxima.tile([P, P], F32)
+                nc.vector.tensor_reduce(
+                    out=top[:], in_=k_acc[h][:].rearrange("p b c -> p c b"), axis=mybir.AxisListType.X, op=mybir.AluOpType.max
+                )
+                tops.append(top)
+            for h in range(HALVES):
+                e_half = e_tile[:, :, jj, h * P : (h + 1) * P]
+                nc.vector.tensor_tensor(
+                    out=e_half, in0=k_acc[h][:], in1=tops[h][:].unsqueeze(1).to_broadcast([P, B, P]), op=mybir.AluOpType.subtract
+                )
+                nc.scalar.activation(out=e_half, in_=e_half, func=mybir.ActivationFunctionType.Exp)
+            store(e_rows, e_tile, g)
+
+            if g + 1 < STEPS:
+                k_acc = project(psum_k, quantise(stage, k_grouped[g + 1], "k"), 0)
+                v_operand = quantise(stage, v_grouped[g + 1], "v")
+
+            v_half = stage.tile([P, B, P], F32)
+            nc.scalar.copy(out=v_half[:], in_=v_acc[1][:])
+            nc.gpsimd.tensor_tensor(
+                out=ev_tile[:, :, jj, P : 2 * P], in0=v_half[:], in1=e_tile[:, :, jj, P : 2 * P], op=mybir.AluOpType.mult
+            )
+            if ahead < STEPS:
+                v_grouped[ahead] = regroup(v_banks, "v")
+            nc.vector.tensor_tensor(
+                out=ev_tile[:, :, jj, 0:P], in0=v_acc[0][:], in1=e_tile[:, :, jj, 0:P], op=mybir.AluOpType.mult
+            )
+            store(ev_rows, ev_tile, g)

@@ -15,12 +15,12 @@ B, T, DM, DH = 4, 2048, 512, 256
 WORDS = DM // 2
 HALVES = DH // P
 STEPS = T // P
-J_LOAD = 2
+J_LOAD = 4
 J_STORE = 4
-LOAD_BUFS = 4
+LOAD_BUFS = 3
 STORE_BUFS = 3
 CHUNKS = STEPS // J_LOAD
-HEAD_CHUNKS = 2
+PIECES = {0: 1, 1: 2}
 
 FLOPS = 2 * 2 * B * T * DM * DH
 
@@ -47,14 +47,13 @@ def tile_aftfull_pa_t_kernel(tc, k, v, Wk, Wv, out_0, out_1):
         v_chunks = {}
 
         def fetch(c):
-            k_chunk = loads.tile([P, B, J_LOAD, DM], BF16)
-            v_chunk = loads.tile([P, B, J_LOAD, DM], BF16)
-            piece = 1 if c < HEAD_CHUNKS else J_LOAD
-            for first in range(0, J_LOAD, piece):
-                inside = slice(first, first + piece)
-                steps = slice(c * J_LOAD + first, c * J_LOAD + first + piece)
-                nc.sync.dma_start(out=k_chunk[:, :, inside, :], in_=k_rows[:, :, steps, :])
-                nc.sync.dma_start(out=v_chunk[:, :, inside, :], in_=v_rows[:, :, steps, :])
+            piece = PIECES.get(c, J_LOAD)
+            k_chunk = loads.tile([P, J_LOAD // piece, B, piece, DM], BF16)
+            v_chunk = loads.tile([P, J_LOAD // piece, B, piece, DM], BF16)
+            for i in range(J_LOAD // piece):
+                steps = slice(c * J_LOAD + i * piece, c * J_LOAD + (i + 1) * piece)
+                nc.sync.dma_start(out=k_chunk[:, i, :, :, :], in_=k_rows[:, :, steps, :])
+                nc.sync.dma_start(out=v_chunk[:, i, :, :, :], in_=v_rows[:, :, steps, :])
             k_chunks[c] = k_chunk
             v_chunks[c] = v_chunk
 
@@ -64,8 +63,10 @@ def tile_aftfull_pa_t_kernel(tc, k, v, Wk, Wv, out_0, out_1):
 
         def store(rows, result, g):
             jj = g % J_STORE
-            if g >= STEPS - J_STORE:
+            if g >= STEPS - 2:
                 lo, hi = jj, jj + 1
+            elif g == STEPS - 3:
+                lo, hi = 0, jj + 1
             elif jj == J_STORE - 1:
                 lo, hi = 0, J_STORE
             else:
@@ -73,8 +74,10 @@ def tile_aftfull_pa_t_kernel(tc, k, v, Wk, Wv, out_0, out_1):
             nc.sync.dma_start(out=rows[:, :, g - jj + lo : g - jj + hi, :], in_=result[:, :, lo:hi, :])
 
         def rows_of_step(chunks, g):
-            words = chunks[g // J_LOAD][:].bitcast(F32)
-            return [words[:, b, g % J_LOAD, :] for b in range(B)]
+            c = g // J_LOAD
+            i, j = divmod(g % J_LOAD, PIECES.get(c, J_LOAD))
+            words = chunks[c][:].bitcast(F32)
+            return [words[:, i, b, j, :] for b in range(B)]
 
         def transpose_rows(rows):
             banks = []
@@ -134,7 +137,7 @@ def tile_aftfull_pa_t_kernel(tc, k, v, Wk, Wv, out_0, out_1):
             fetch(c)
 
         w_words = w_raw[:].bitcast(F32)
-        w_grouped = regroup(transpose_rows([w_words[:, i, :] for i in range(2 * HALVES)]), "w")
+        w_grouped = regroup(transpose_rows([w_words[:, i, :] for i in range(2 * HALVES)]), "k")
         w_codes, w_scales = quantise(consts, w_grouped, "w")
 
         k_grouped = {}

@@ -15,14 +15,25 @@ B, T, DM, DH = 4, 2048, 512, 256
 WORDS = DM // 2
 HALVES = DH // P
 STEPS = T // P
-J_LOAD = 4
-J_STORE = 4
+RUNS = P // B
+QUARTERS = P // RUNS
+
+CHUNKS = ((1, 1, 2), (2, 2), (4,), (4,))
+J_CHUNK = 4
 LOAD_BUFS = 3
 STORE_BUFS = 3
-CHUNKS = STEPS // J_LOAD
-PIECES = {0: 1, 1: 2}
+HEAD_STEPS = 2
+LAST_STORES = (2, 1, 1)
 
 FLOPS = 2 * 2 * B * T * DM * DH
+
+
+def spans(lengths, first):
+    out = []
+    for n in lengths:
+        out.append((first, n))
+        first += n
+    return out
 
 
 def tile_aftfull_pa_t_kernel(tc, k, v, Wk, Wv, out_0, out_1):
@@ -38,71 +49,94 @@ def tile_aftfull_pa_t_kernel(tc, k, v, Wk, Wv, out_0, out_1):
         psum_v = ctx.enter_context(tc.psum_pool(name="psum_v", bufs=HALVES))
         ctx.enter_context(tc.manual_schedule())
 
-        k_rows = k.rearrange("b (p j) d -> p b j d", j=STEPS)
-        v_rows = v.rearrange("b (p j) d -> p b j d", j=STEPS)
-        ev_rows = out_0.rearrange("b (p j) c -> p b j c", j=STEPS)
-        e_rows = out_1.rearrange("b (p j) c -> p b j c", j=STEPS)
+        k_rows = k.rearrange("b (q j) d -> (b q) j d", q=RUNS)
+        v_rows = v.rearrange("b (q j) d -> (b q) j d", q=RUNS)
+        ev_rows = out_0.rearrange("b (q j) c -> q b j c", q=RUNS)
+        e_rows = out_1.rearrange("b (q j) c -> q b j c", q=RUNS)
 
-        k_chunks = {}
-        v_chunks = {}
+        groups = {}
+        for c, lengths in enumerate(CHUNKS):
+            for first, n in spans(lengths, c * J_CHUNK):
+                for g in range(first, first + n):
+                    groups[g] = (first, n)
+        pieces = []
+        for c, lengths in enumerate(CHUNKS):
+            pieces += spans(LAST_STORES if c == len(CHUNKS) - 1 else lengths, c * J_CHUNK)
+
+        inputs = {}
+        e_pieces = {}
+        ev_pieces = {}
+        e_steps = {}
+        ev_steps = {}
 
         def fetch(c):
-            piece = PIECES.get(c, J_LOAD)
-            k_chunk = loads.tile([P, J_LOAD // piece, B, piece, DM], BF16)
-            v_chunk = loads.tile([P, J_LOAD // piece, B, piece, DM], BF16)
-            for i in range(J_LOAD // piece):
-                steps = slice(c * J_LOAD + i * piece, c * J_LOAD + (i + 1) * piece)
-                nc.sync.dma_start(out=k_chunk[:, i, :, :, :], in_=k_rows[:, :, steps, :])
-                nc.sync.dma_start(out=v_chunk[:, i, :, :, :], in_=v_rows[:, :, steps, :])
-            k_chunks[c] = k_chunk
-            v_chunks[c] = v_chunk
+            k_chunk = loads.tile([P, J_CHUNK * QUARTERS * DM], BF16)
+            v_chunk = loads.tile([P, J_CHUNK * QUARTERS * DM], BF16)
+            for first, n in spans(CHUNKS[c], c * J_CHUNK):
+                lo = (first - c * J_CHUNK) * QUARTERS * DM
+                for which, rows, chunk in (("k", k_rows, k_chunk), ("v", v_rows, v_chunk)):
+                    run = chunk[:, lo : lo + n * QUARTERS * DM]
+                    tokens = rows[:, first * QUARTERS : (first + n) * QUARTERS, :]
+                    nc.sync.dma_start(out=run.rearrange("p (t d) -> p t d", d=DM), in_=tokens)
+                    by_step = run.bitcast(F32).rearrange("p (jj i w) -> p i jj w", jj=QUARTERS, i=n)
+                    for i in range(n):
+                        inputs[which, first + i] = by_step[:, i, :, :]
 
         def refill_after(g):
-            if g % J_LOAD == J_LOAD - 1 and g // J_LOAD + LOAD_BUFS < CHUNKS:
-                fetch(g // J_LOAD + LOAD_BUFS)
+            if g % J_CHUNK == J_CHUNK - 1 and g // J_CHUNK + LOAD_BUFS < len(CHUNKS):
+                fetch(g // J_CHUNK + LOAD_BUFS)
 
-        def store(rows, result, g):
-            jj = g % J_STORE
-            if g >= STEPS - 2:
-                lo, hi = jj, jj + 1
-            elif g == STEPS - 3:
-                lo, hi = 0, jj + 1
-            elif jj == J_STORE - 1:
-                lo, hi = 0, J_STORE
-            else:
+        def open_results(g):
+            if g % J_CHUNK:
                 return
-            nc.sync.dma_start(out=rows[:, :, g - jj + lo : g - jj + hi, :], in_=result[:, :, lo:hi, :])
+            e_tile = results.tile([P, J_CHUNK * B * DH], F32)
+            ev_tile = results.tile([P, J_CHUNK * B * DH], F32)
+            for first, n in pieces:
+                if g <= first < g + J_CHUNK:
+                    lo = (first - g) * B * DH
+                    hi = lo + n * B * DH
+                    e_pieces[first] = e_tile[:, lo:hi].rearrange("p (b i c) -> p b i c", b=B, i=n)
+                    ev_pieces[first] = ev_tile[:, lo:hi].rearrange("p (b i c) -> p b i c", b=B, i=n)
+                    for i in range(n):
+                        e_steps[first + i] = e_pieces[first][:, :, i, :]
+                        ev_steps[first + i] = ev_pieces[first][:, :, i, :]
 
-        def rows_of_step(chunks, g):
-            c = g // J_LOAD
-            i, j = divmod(g % J_LOAD, PIECES.get(c, J_LOAD))
-            words = chunks[c][:].bitcast(F32)
-            return [words[:, i, b, j, :] for b in range(B)]
+        def store(rows, stored, g):
+            for first, n in pieces:
+                if g == first + n - 1:
+                    group_first, group_n = groups[first]
+                    for jj in range(QUARTERS):
+                        token = group_first * QUARTERS + jj * group_n + first - group_first
+                        nc.sync.dma_start(out=rows[:, :, token : token + n, :], in_=stored[first][jj:P:QUARTERS, :, :, :])
 
-        def transpose_rows(rows):
+        def transpose_rows(blocks):
             banks = []
             for pair in range(2):
                 xt = psum_t.tile([P, 2, 2, P], F32)
                 for i in range(2):
                     for u in range(2):
-                        nc.tensor.transpose(xt[:, i, u, :], rows[2 * pair + i][:, u:WORDS:2], identity[:])
+                        nc.tensor.transpose(xt[:, i, u, :], blocks[2 * pair + i][:, u:WORDS:2], identity[:])
                 banks.append(xt)
             return banks
 
-        def regroup(banks, which):
-            grouped = stage.tile([P, B, P, PACK], BF16, tag="grouped_" + which, align_bytes=64)
+        def regroup(bank, words):
+            nc.scalar.copy(out=words, in_=bank[:].rearrange("p i u r -> p r i u"))
+
+        def regroup_step(banks, which):
+            grouped = stage.tile([P, P, QUARTERS, PACK], BF16, tag="grouped_" + which, align_bytes=64)
             words = grouped[:].bitcast(F32)
             for pair in range(2):
-                nc.scalar.copy(out=words[:, 2 * pair : 2 * pair + 2, :, :], in_=banks[pair][:].rearrange("p i u r -> p i r u"))
+                regroup(banks[pair], words[:, :, 2 * pair : 2 * pair + 2, :])
             return grouped
 
         def quantise(pool, grouped, which):
             codes = pool.tile([P, B * P], U32, tag="codes_" + which, align_bytes=64)
             scales = pool.tile([P, B * P], U8, tag="scales_" + which, align_bytes=64)
-            nc.vector.quantize_mx(
-                out=codes[:].bitcast(FP8X4), scales=scales[:], in_=grouped[:].rearrange("p b r t -> p (b r t)")
-            )
+            nc.vector.quantize_mx(out=codes[:].bitcast(FP8X4), scales=scales[:], in_=grouped)
             return codes, scales
+
+        def quantise_step(grouped, which):
+            return quantise(stage, grouped[:].rearrange("p r j t -> p (r j t)"), which)
 
         def project(pool, operand, first_w_block):
             codes, scales = operand
@@ -124,6 +158,9 @@ def tile_aftfull_pa_t_kernel(tc, k, v, Wk, Wv, out_0, out_1):
                 accs.append(acc)
             return accs
 
+        def rows_of_step(which, g):
+            return [inputs[which, g][:, jj, :] for jj in range(QUARTERS)]
+
         identity = consts.tile([P, P], F32)
         make_identity(nc, identity[:])
         warm = consts.tile([P, 1], F32)
@@ -131,38 +168,39 @@ def tile_aftfull_pa_t_kernel(tc, k, v, Wk, Wv, out_0, out_1):
         nc.scalar.activation(out=warm[:], in_=warm[:], func=mybir.ActivationFunctionType.Exp)
 
         w_raw = consts.tile([P, 2 * HALVES, DM], BF16)
-        nc.sync.dma_start(out=w_raw[:, 0:HALVES, :], in_=Wk.rearrange("(i p) d -> p i d", p=P))
-        nc.sync.dma_start(out=w_raw[:, HALVES : 2 * HALVES, :], in_=Wv.rearrange("(i p) d -> p i d", p=P))
+        nc.sync.dma_start(out=w_raw[:, 0:HALVES, :], in_=Wk.rearrange("(p i) d -> p i d", p=P))
+        nc.sync.dma_start(out=w_raw[:, HALVES : 2 * HALVES, :], in_=Wv.rearrange("(p i) d -> p i d", p=P))
         for c in range(LOAD_BUFS):
             fetch(c)
 
         w_words = w_raw[:].bitcast(F32)
-        w_grouped = regroup(transpose_rows([w_words[:, i, :] for i in range(2 * HALVES)]), "k")
-        w_codes, w_scales = quantise(consts, w_grouped, "w")
+        w_banks = transpose_rows([w_words[:, i, :] for i in range(2 * HALVES)])
+        w_grouped = stage.tile([P, 2, P, HALVES, PACK], BF16, tag="grouped_k", align_bytes=64)
+        for which in range(2):
+            regroup(w_banks[which], w_grouped[:].bitcast(F32)[:, which, :, :, :])
+        w_codes, w_scales = quantise(consts, w_grouped[:].rearrange("p w r i t -> p (w r i t)"), "w")
 
         k_grouped = {}
         v_grouped = {}
-        k_grouped[0] = regroup(transpose_rows(rows_of_step(k_chunks, 0)), "k")
-        v_grouped[0] = regroup(transpose_rows(rows_of_step(v_chunks, 0)), "v")
-        k_acc = project(psum_k, quantise(stage, k_grouped[0], "k"), 0)
-        v_operand = quantise(stage, v_grouped[0], "v")
-        k_grouped[1] = regroup(transpose_rows(rows_of_step(k_chunks, 1)), "k")
-        v_grouped[1] = regroup(transpose_rows(rows_of_step(v_chunks, 1)), "v")
-        refill_after(0)
-        refill_after(1)
+        k_grouped[0] = regroup_step(transpose_rows(rows_of_step("k", 0)), "k")
+        v_grouped[0] = regroup_step(transpose_rows(rows_of_step("v", 0)), "v")
+        k_acc = project(psum_k, quantise_step(k_grouped[0], "k"), 0)
+        v_operand = quantise_step(v_grouped[0], "v")
+        k_grouped[1] = regroup_step(transpose_rows(rows_of_step("k", 1)), "k")
+        v_grouped[1] = regroup_step(transpose_rows(rows_of_step("v", 1)), "v")
 
         for g in range(STEPS):
             ahead = g + 2
-            jj = g % J_STORE
-            if jj == 0:
-                e_tile = results.tile([P, B, J_STORE, DH], F32)
-                ev_tile = results.tile([P, B, J_STORE, DH], F32)
+            open_results(g)
 
+            if g < HEAD_STEPS:
+                v_acc = project(psum_v, v_operand, HALVES)
             if ahead < STEPS:
-                k_grouped[ahead] = regroup(transpose_rows(rows_of_step(k_chunks, ahead)), "k")
-                v_banks = transpose_rows(rows_of_step(v_chunks, ahead))
+                k_grouped[ahead] = regroup_step(transpose_rows(rows_of_step("k", ahead)), "k")
+                v_banks = transpose_rows(rows_of_step("v", ahead))
                 refill_after(ahead)
-            v_acc = project(psum_v, v_operand, HALVES)
+            if g >= HEAD_STEPS:
+                v_acc = project(psum_v, v_operand, HALVES)
 
             tops = []
             for h in range(HALVES):
@@ -172,25 +210,25 @@ def tile_aftfull_pa_t_kernel(tc, k, v, Wk, Wv, out_0, out_1):
                 )
                 tops.append(top)
             for h in range(HALVES):
-                e_half = e_tile[:, :, jj, h * P : (h + 1) * P]
+                e_half = e_steps[g][:, :, h * P : (h + 1) * P]
                 nc.vector.tensor_tensor(
                     out=e_half, in0=k_acc[h][:], in1=tops[h][:].unsqueeze(1).to_broadcast([P, B, P]), op=mybir.AluOpType.subtract
                 )
                 nc.scalar.activation(out=e_half, in_=e_half, func=mybir.ActivationFunctionType.Exp)
-            store(e_rows, e_tile, g)
+            store(e_rows, e_pieces, g)
 
             if g + 1 < STEPS:
-                k_acc = project(psum_k, quantise(stage, k_grouped[g + 1], "k"), 0)
-                v_operand = quantise(stage, v_grouped[g + 1], "v")
+                k_acc = project(psum_k, quantise_step(k_grouped[g + 1], "k"), 0)
+                v_operand = quantise_step(v_grouped[g + 1], "v")
 
             v_half = stage.tile([P, B, P], F32)
             nc.scalar.copy(out=v_half[:], in_=v_acc[1][:])
             nc.gpsimd.tensor_tensor(
-                out=ev_tile[:, :, jj, P : 2 * P], in0=v_half[:], in1=e_tile[:, :, jj, P : 2 * P], op=mybir.AluOpType.mult
+                out=ev_steps[g][:, :, P : 2 * P], in0=v_half[:], in1=e_steps[g][:, :, P : 2 * P], op=mybir.AluOpType.mult
             )
             if ahead < STEPS:
-                v_grouped[ahead] = regroup(v_banks, "v")
+                v_grouped[ahead] = regroup_step(v_banks, "v")
             nc.vector.tensor_tensor(
-                out=ev_tile[:, :, jj, 0:P], in0=v_acc[0][:], in1=e_tile[:, :, jj, 0:P], op=mybir.AluOpType.mult
+                out=ev_steps[g][:, :, 0:P], in0=v_acc[0][:], in1=e_steps[g][:, :, 0:P], op=mybir.AluOpType.mult
             )
-            store(ev_rows, ev_tile, g)
+            store(ev_rows, ev_pieces, g)

@@ -22,7 +22,6 @@ CHUNKS = ((1, 1, 2), (2, 2), (4,), (4,))
 J_CHUNK = 4
 LOAD_BUFS = 3
 STORE_BUFS = 3
-HEAD_STEPS = 2
 LAST_STORES = (2, 1, 1)
 
 FLOPS = 2 * 2 * B * T * DM * DH
@@ -69,12 +68,17 @@ def tile_aftfull_pa_t_kernel(tc, k, v, Wk, Wv, out_0, out_1):
         e_steps = {}
         ev_steps = {}
 
-        def fetch(c):
+        def load_weights(raw, w):
+            nc.sync.dma_start(out=raw[:], in_=w.rearrange("(p i) d -> p i d", p=P))
+
+        def fetch(c, weights=None):
             k_chunk = loads.tile([P, J_CHUNK * QUARTERS * DM], BF16)
             v_chunk = loads.tile([P, J_CHUNK * QUARTERS * DM], BF16)
             for first, n in spans(CHUNKS[c], c * J_CHUNK):
                 lo = (first - c * J_CHUNK) * QUARTERS * DM
                 for which, rows, chunk in (("k", k_rows, k_chunk), ("v", v_rows, v_chunk)):
+                    if weights and first == 0:
+                        load_weights(*weights[which])
                     run = chunk[:, lo : lo + n * QUARTERS * DM]
                     tokens = rows[:, first * QUARTERS : (first + n) * QUARTERS, :]
                     nc.sync.dma_start(out=run.rearrange("p (t d) -> p t d", d=DM), in_=tokens)
@@ -109,15 +113,22 @@ def tile_aftfull_pa_t_kernel(tc, k, v, Wk, Wv, out_0, out_1):
                         token = group_first * QUARTERS + jj * group_n + first - group_first
                         nc.sync.dma_start(out=rows[:, :, token : token + n, :], in_=stored[first][jj:P:QUARTERS, :, :, :])
 
-        def transpose_rows(blocks):
-            banks = []
-            for pair in range(2):
-                xt = psum_t.tile([P, 2, 2, P], F32)
-                for i in range(2):
-                    for u in range(2):
-                        nc.tensor.transpose(xt[:, i, u, :], blocks[2 * pair + i][:, u:WORDS:2], identity[:])
-                banks.append(xt)
-            return banks
+        def transpose_pair(blocks):
+            bank = psum_t.tile([P, 2, 2, P], F32)
+            for i in range(2):
+                for u in range(2):
+                    nc.tensor.transpose(bank[:, i, u, :], blocks[:, i, u:WORDS:2], identity[:])
+            return bank
+
+        def transpose_step(which, g):
+            return [transpose_pair(inputs[which, g][:, jj : jj + 2, :]) for jj in range(0, QUARTERS, 2)]
+
+        def transpose_weights(raw):
+            return transpose_pair(raw[:].bitcast(F32))
+
+        def weight_tile():
+            w_grouped = stage.tile([P, P, HALVES, PACK], BF16, align_bytes=64)
+            return w_grouped
 
         def regroup(bank, words):
             nc.scalar.copy(out=words, in_=bank[:].rearrange("p i u r -> p r i u"))
@@ -129,21 +140,22 @@ def tile_aftfull_pa_t_kernel(tc, k, v, Wk, Wv, out_0, out_1):
                 regroup(banks[pair], words[:, :, 2 * pair : 2 * pair + 2, :])
             return grouped
 
-        def quantise(pool, grouped, which):
-            codes = pool.tile([P, B * P], U32, tag="codes_" + which, align_bytes=64)
-            scales = pool.tile([P, B * P], U8, tag="scales_" + which, align_bytes=64)
+        def quantise(pool, grouped, columns, which):
+            codes = pool.tile([P, columns], U32, tag="codes_" + which, align_bytes=64)
+            scales = pool.tile([P, columns], U8, tag="scales_" + which, align_bytes=64)
             nc.vector.quantize_mx(out=codes[:].bitcast(FP8X4), scales=scales[:], in_=grouped)
             return codes, scales
 
         def quantise_step(grouped, which):
-            return quantise(stage, grouped[:].rearrange("p r j t -> p (r j t)"), which)
+            return quantise(stage, grouped[:].rearrange("p r j t -> p (r j t)"), B * P, which)
 
-        def project(pool, operand, first_w_block):
+        def project(pool, operand, weights):
             codes, scales = operand
+            w_codes, w_scales = weights
             accs = []
             for h in range(HALVES):
                 acc = pool.tile([P, B, P], F32)
-                w_cols = slice((first_w_block + h) * P, (first_w_block + h + 1) * P)
+                w_cols = slice(h * P, (h + 1) * P)
                 for b in range(B):
                     tokens = slice(b * P, (b + 1) * P)
                     nc.tensor.matmul_mx(
@@ -158,8 +170,11 @@ def tile_aftfull_pa_t_kernel(tc, k, v, Wk, Wv, out_0, out_1):
                 accs.append(acc)
             return accs
 
-        def rows_of_step(which, g):
-            return [inputs[which, g][:, jj, :] for jj in range(QUARTERS)]
+        def times_v_on_vector(g, v_acc, h):
+            channels = slice(h * P, (h + 1) * P)
+            nc.vector.tensor_tensor(
+                out=ev_steps[g][:, :, channels], in0=v_acc[h][:], in1=e_steps[g][:, :, channels], op=mybir.AluOpType.mult
+            )
 
         identity = consts.tile([P, P], F32)
         make_identity(nc, identity[:])
@@ -167,40 +182,40 @@ def tile_aftfull_pa_t_kernel(tc, k, v, Wk, Wv, out_0, out_1):
         nc.vector.memset(warm[:], 0.0)
         nc.scalar.activation(out=warm[:], in_=warm[:], func=mybir.ActivationFunctionType.Exp)
 
-        w_raw = consts.tile([P, 2 * HALVES, DM], BF16)
-        nc.sync.dma_start(out=w_raw[:, 0:HALVES, :], in_=Wk.rearrange("(p i) d -> p i d", p=P))
-        nc.sync.dma_start(out=w_raw[:, HALVES : 2 * HALVES, :], in_=Wv.rearrange("(p i) d -> p i d", p=P))
-        for c in range(LOAD_BUFS):
+        wk_raw = consts.tile([P, HALVES, DM], BF16)
+        wv_raw = consts.tile([P, HALVES, DM], BF16)
+        fetch(0, weights={"k": (wk_raw, Wk), "v": (wv_raw, Wv)})
+        for c in range(1, LOAD_BUFS):
             fetch(c)
 
-        w_words = w_raw[:].bitcast(F32)
-        w_banks = transpose_rows([w_words[:, i, :] for i in range(2 * HALVES)])
-        w_grouped = stage.tile([P, 2, P, HALVES, PACK], BF16, tag="grouped_k", align_bytes=64)
-        for which in range(2):
-            regroup(w_banks[which], w_grouped[:].bitcast(F32)[:, which, :, :, :])
-        w_codes, w_scales = quantise(consts, w_grouped[:].rearrange("p w r i t -> p (w r i t)"), "w")
-
-        k_grouped = {}
-        v_grouped = {}
-        k_grouped[0] = regroup_step(transpose_rows(rows_of_step("k", 0)), "k")
-        v_grouped[0] = regroup_step(transpose_rows(rows_of_step("v", 0)), "v")
-        k_acc = project(psum_k, quantise_step(k_grouped[0], "k"), 0)
-        v_operand = quantise_step(v_grouped[0], "v")
-        k_grouped[1] = regroup_step(transpose_rows(rows_of_step("k", 1)), "k")
-        v_grouped[1] = regroup_step(transpose_rows(rows_of_step("v", 1)), "v")
+        wk_bank = transpose_weights(wk_raw)
+        wk_grouped = weight_tile()
+        nc.vector.tensor_copy(out=wk_grouped[:].bitcast(F32), in_=wk_bank[:].rearrange("p i u r -> p r i u"))
+        wk = quantise(consts, wk_grouped[:].rearrange("p r i t -> p (r i t)"), DH, "wk")
+        k_grouped = {0: regroup_step(transpose_step("k", 0), "k")}
+        k_operand = quantise_step(k_grouped[0], "k")
+        wv_bank = transpose_weights(wv_raw)
+        wv_grouped = weight_tile()
+        regroup(wv_bank, wv_grouped[:].bitcast(F32))
+        v_grouped = {0: regroup_step(transpose_step("v", 0), "v")}
+        k_acc = project(psum_k, k_operand, wk)
+        wv = quantise(consts, wv_grouped[:].rearrange("p r i t -> p (r i t)"), DH, "wv")
+        k_grouped[1] = regroup_step(transpose_step("k", 1), "k")
+        v_grouped[1] = regroup_step(transpose_step("v", 1), "v")
+        v_operand = None
 
         for g in range(STEPS):
             ahead = g + 2
+            first = g == 0
+            last = g == STEPS - 1
             open_results(g)
 
-            if g < HEAD_STEPS:
-                v_acc = project(psum_v, v_operand, HALVES)
-            if ahead < STEPS:
-                k_grouped[ahead] = regroup_step(transpose_rows(rows_of_step("k", ahead)), "k")
-                v_banks = transpose_rows(rows_of_step("v", ahead))
+            if ahead < STEPS and not first:
+                k_grouped[ahead] = regroup_step(transpose_step("k", ahead), "k")
+                v_banks = transpose_step("v", ahead)
                 refill_after(ahead)
-            if g >= HEAD_STEPS:
-                v_acc = project(psum_v, v_operand, HALVES)
+            if not first:
+                v_acc = project(psum_v, v_operand, wv)
 
             tops = []
             for h in range(HALVES):
@@ -209,6 +224,8 @@ def tile_aftfull_pa_t_kernel(tc, k, v, Wk, Wv, out_0, out_1):
                     out=top[:], in_=k_acc[h][:].rearrange("p b c -> p c b"), axis=mybir.AxisListType.X, op=mybir.AluOpType.max
                 )
                 tops.append(top)
+            if first:
+                v_acc = project(psum_v, quantise_step(v_grouped[0], "v"), wv)
             for h in range(HALVES):
                 e_half = e_steps[g][:, :, h * P : (h + 1) * P]
                 nc.vector.tensor_tensor(
@@ -217,18 +234,26 @@ def tile_aftfull_pa_t_kernel(tc, k, v, Wk, Wv, out_0, out_1):
                 nc.scalar.activation(out=e_half, in_=e_half, func=mybir.ActivationFunctionType.Exp)
             store(e_rows, e_pieces, g)
 
-            if g + 1 < STEPS:
-                k_acc = project(psum_k, quantise_step(k_grouped[g + 1], "k"), 0)
-                v_operand = quantise_step(v_grouped[g + 1], "v")
+            if not last:
+                k_acc = project(psum_k, quantise_step(k_grouped[g + 1], "k"), wk)
+                if not first:
+                    v_operand = quantise_step(v_grouped[g + 1], "v")
 
-            v_half = stage.tile([P, B, P], F32)
-            nc.scalar.copy(out=v_half[:], in_=v_acc[1][:])
-            nc.gpsimd.tensor_tensor(
-                out=ev_steps[g][:, :, P : 2 * P], in0=v_half[:], in1=e_steps[g][:, :, P : 2 * P], op=mybir.AluOpType.mult
-            )
-            if ahead < STEPS:
-                v_grouped[ahead] = regroup_step(v_banks, "v")
-            nc.vector.tensor_tensor(
-                out=ev_steps[g][:, :, 0:P], in0=v_acc[0][:], in1=e_steps[g][:, :, 0:P], op=mybir.AluOpType.mult
-            )
+            if last:
+                times_v_on_vector(g, v_acc, 0)
+                times_v_on_vector(g, v_acc, 1)
+            else:
+                v_half = stage.tile([P, B, P], F32)
+                nc.scalar.copy(out=v_half[:], in_=v_acc[1][:])
+                nc.gpsimd.tensor_tensor(
+                    out=ev_steps[g][:, :, P : 2 * P], in0=v_half[:], in1=e_steps[g][:, :, P : 2 * P], op=mybir.AluOpType.mult
+                )
+                if first:
+                    k_grouped[ahead] = regroup_step(transpose_step("k", ahead), "k")
+                    v_banks = transpose_step("v", ahead)
+                if ahead < STEPS:
+                    v_grouped[ahead] = regroup_step(v_banks, "v")
+                times_v_on_vector(g, v_acc, 0)
+                if first:
+                    v_operand = quantise_step(v_grouped[1], "v")
             store(ev_rows, ev_pieces, g)

@@ -212,10 +212,11 @@ def tile_aftfull_pa_t_kernel(tc, k, v, Wk, Wv, out_0, out_1):
 
             if ahead < STEPS and not first:
                 k_grouped[ahead] = regroup_step(transpose_step("k", ahead), "k")
-                v_banks = transpose_step("v", ahead)
-                refill_after(ahead)
             if not first:
                 v_acc = project(psum_v, v_operand, wv)
+            if ahead < STEPS and not first:
+                v_banks = transpose_step("v", ahead)
+                refill_after(ahead)
 
             tops = []
             for h in range(HALVES):

@@ -22,6 +22,7 @@ CHUNKS = ((1, 1, 2), (2, 2), (4,), (4,))
 J_CHUNK = 4
 LOAD_BUFS = 3
 STORE_BUFS = 3
+E_SPLIT = {2: (2, 2)}
 LAST_STORES = (2, 1, 1)
 
 FLOPS = 2 * 2 * B * T * DM * DH
@@ -58,9 +59,12 @@ def tile_aftfull_pa_t_kernel(tc, k, v, Wk, Wv, out_0, out_1):
             for first, n in spans(lengths, c * J_CHUNK):
                 for g in range(first, first + n):
                     groups[g] = (first, n)
-        pieces = []
+        ev_pieces_of = []
+        e_pieces_of = []
         for c, lengths in enumerate(CHUNKS):
-            pieces += spans(LAST_STORES if c == len(CHUNKS) - 1 else lengths, c * J_CHUNK)
+            last_chunk = c == len(CHUNKS) - 1
+            ev_pieces_of += spans(LAST_STORES if last_chunk else lengths, c * J_CHUNK)
+            e_pieces_of += spans(LAST_STORES if last_chunk else E_SPLIT.get(c, lengths), c * J_CHUNK)
 
         inputs = {}
         e_pieces = {}
@@ -95,18 +99,19 @@ def tile_aftfull_pa_t_kernel(tc, k, v, Wk, Wv, out_0, out_1):
                 return
             e_tile = results.tile([P, J_CHUNK * B * DH], F32)
             ev_tile = results.tile([P, J_CHUNK * B * DH], F32)
-            for first, n in pieces:
-                if g <= first < g + J_CHUNK:
-                    lo = (first - g) * B * DH
-                    hi = lo + n * B * DH
-                    e_pieces[first] = e_tile[:, lo:hi].rearrange("p (b i c) -> p b i c", b=B, i=n)
-                    ev_pieces[first] = ev_tile[:, lo:hi].rearrange("p (b i c) -> p b i c", b=B, i=n)
-                    for i in range(n):
-                        e_steps[first + i] = e_pieces[first][:, :, i, :]
-                        ev_steps[first + i] = ev_pieces[first][:, :, i, :]
+            for tile, lengths, by_piece, by_step in (
+                (e_tile, e_pieces_of, e_pieces, e_steps),
+                (ev_tile, ev_pieces_of, ev_pieces, ev_steps),
+            ):
+                for first, n in lengths:
+                    if g <= first < g + J_CHUNK:
+                        run = tile[:, (first - g) * B * DH : (first - g + n) * B * DH]
+                        by_piece[first] = run.rearrange("p (b i c) -> p b i c", b=B, i=n)
+                        for i in range(n):
+                            by_step[first + i] = by_piece[first][:, :, i, :]
 
-        def store(rows, stored, g):
-            for first, n in pieces:
+        def store(rows, lengths, stored, g):
+            for first, n in lengths:
                 if g == first + n - 1:
                     group_first, group_n = groups[first]
                     for jj in range(QUARTERS):
@@ -233,7 +238,7 @@ def tile_aftfull_pa_t_kernel(tc, k, v, Wk, Wv, out_0, out_1):
                     out=e_half, in0=k_acc[h][:], in1=tops[h][:].unsqueeze(1).to_broadcast([P, B, P]), op=mybir.AluOpType.subtract
                 )
                 nc.scalar.activation(out=e_half, in_=e_half, func=mybir.ActivationFunctionType.Exp)
-            store(e_rows, e_pieces, g)
+            store(e_rows, e_pieces_of, e_pieces, g)
 
             if not last:
                 k_acc = project(psum_k, quantise_step(k_grouped[g + 1], "k"), wk)
@@ -257,4 +262,4 @@ def tile_aftfull_pa_t_kernel(tc, k, v, Wk, Wv, out_0, out_1):
                 times_v_on_vector(g, v_acc, 0)
                 if first:
                     v_operand = quantise_step(v_grouped[1], "v")
-            store(ev_rows, ev_pieces, g)
+            store(ev_rows, ev_pieces_of, ev_pieces, g)

from contextlib import ExitStack

import concourse.mybir as mybir
from concourse.masks import make_identity

F32 = mybir.dt.float32
BF16 = mybir.dt.bfloat16
U32 = mybir.dt.uint32
U8 = mybir.dt.uint8
FP8X4 = mybir.dt.float8_e4m3fn_x4

P = 128
PACK = 4
B, T, DM, DH = 4, 2048, 512, 256
WORDS = DM // 2
HALVES = DH // P
STEPS = T // P
RUNS = P // B
QUARTERS = P // RUNS

CHUNKS = ((1, 1, 2), (2, 2), (4,), (4,))
J_CHUNK = 4
LOAD_BUFS = 3
STORE_BUFS = 3
E_SPLIT = {2: (2, 2)}
LAST_STORES = (2, 1, 1)

FLOPS = 2 * 2 * B * T * DM * DH


def spans(lengths, first):
    out = []
    for n in lengths:
        out.append((first, n))
        first += n
    return out


def tile_aftfull_pa_t_kernel(tc, k, v, Wk, Wv, out_0, out_1):
    nc = tc.nc
    with ExitStack() as ctx:
        consts = ctx.enter_context(tc.tile_pool(name="consts", bufs=1))
        loads = ctx.enter_context(tc.tile_pool(name="loads", bufs=LOAD_BUFS))
        stage = ctx.enter_context(tc.tile_pool(name="stage", bufs=2))
        maxima = ctx.enter_context(tc.tile_pool(name="maxima", bufs=2 * HALVES))
        results = ctx.enter_context(tc.tile_pool(name="results", bufs=STORE_BUFS))
        psum_t = ctx.enter_context(tc.psum_pool(name="psum_t", bufs=4))
        psum_k = ctx.enter_context(tc.psum_pool(name="psum_k", bufs=HALVES))
        psum_v = ctx.enter_context(tc.psum_pool(name="psum_v", bufs=HALVES))
        ctx.enter_context(tc.manual_schedule())

        k_rows = k.rearrange("b (q j) d -> (b q) j d", q=RUNS)
        v_rows = v.rearrange("b (q j) d -> (b q) j d", q=RUNS)
        ev_rows = out_0.rearrange("b (q j) c -> q b j c", q=RUNS)
        e_rows = out_1.rearrange("b (q j) c -> q b j c", q=RUNS)

        groups = {}
        for c, lengths in enumerate(CHUNKS):
            for first, n in spans(lengths, c * J_CHUNK):
                for g in range(first, first + n):
                    groups[g] = (first, n)
        ev_pieces_of = []
        e_pieces_of = []
        for c, lengths in enumerate(CHUNKS):
            last_chunk = c == len(CHUNKS) - 1
            ev_pieces_of += spans(LAST_STORES if last_chunk else lengths, c * J_CHUNK)
            e_pieces_of += spans(LAST_STORES if last_chunk else E_SPLIT.get(c, lengths), c * J_CHUNK)

        inputs = {}
        e_pieces = {}
        ev_pieces = {}
        e_steps = {}
        ev_steps = {}

        def load_weights(raw, w):
            nc.sync.dma_start(out=raw[:], in_=w.rearrange("(p i) d -> p i d", p=P))

        def fetch(c, weights=None):
            k_chunk = loads.tile([P, J_CHUNK * QUARTERS * DM], BF16)
            v_chunk = loads.tile([P, J_CHUNK * QUARTERS * DM], BF16)
            for first, n in spans(CHUNKS[c], c * J_CHUNK):
                lo = (first - c * J_CHUNK) * QUARTERS * DM
                for which, rows, chunk in (("k", k_rows, k_chunk), ("v", v_rows, v_chunk)):
                    if weights and first == 0:
                        load_weights(*weights[which])
                    run = chunk[:, lo : lo + n * QUARTERS * DM]
                    tokens = rows[:, first * QUARTERS : (first + n) * QUARTERS, :]
                    nc.sync.dma_start(out=run.rearrange("p (t d) -> p t d", d=DM), in_=tokens)
                    by_step = run.bitcast(F32).rearrange("p (jj i w) -> p i jj w", jj=QUARTERS, i=n)
                    for i in range(n):
                        inputs[which, first + i] = by_step[:, i, :, :]

        def refill_after(g):
            if g % J_CHUNK == J_CHUNK - 1 and g // J_CHUNK + LOAD_BUFS < len(CHUNKS):
                fetch(g // J_CHUNK + LOAD_BUFS)

        def open_results(g):
            if g % J_CHUNK:
                return
            e_tile = results.tile([P, J_CHUNK * B * DH], F32)
            ev_tile = results.tile([P, J_CHUNK * B * DH], F32)
            for tile, lengths, by_piece, by_step in (
                (e_tile, e_pieces_of, e_pieces, e_steps),
                (ev_tile, ev_pieces_of, ev_pieces, ev_steps),
            ):
                for first, n in lengths:
                    if g <= first < g + J_CHUNK:
                        run = tile[:, (first - g) * B * DH : (first - g + n) * B * DH]
                        by_piece[first] = run.rearrange("p (b i c) -> p b i c", b=B, i=n)
                        for i in range(n):
                            by_step[first + i] = by_piece[first][:, :, i, :]

        def store(rows, lengths, stored, g):
            for first, n in lengths:
                if g == first + n - 1:
                    group_first, group_n = groups[first]
                    for jj in range(QUARTERS):
                        token = group_first * QUARTERS + jj * group_n + first - group_first
                        nc.sync.dma_start(out=rows[:, :, token : token + n, :], in_=stored[first][jj:P:QUARTERS, :, :, :])

        def transpose_pair(blocks):
            bank = psum_t.tile([P, 2, 2, P], F32)
            for i in range(2):
                for u in range(2):
                    nc.tensor.transpose(bank[:, i, u, :], blocks[:, i, u:WORDS:2], identity[:])
            return bank

        def transpose_step(which, g):
            return [transpose_pair(inputs[which, g][:, jj : jj + 2, :]) for jj in range(0, QUARTERS, 2)]

        def transpose_weights(raw):
            return transpose_pair(raw[:].bitcast(F32))

        def weight_tile():
            w_grouped = stage.tile([P, P, HALVES, PACK], BF16, align_bytes=64)
            return w_grouped

        def regroup(bank, words):
            nc.scalar.copy(out=words, in_=bank[:].rearrange("p i u r -> p r i u"))

        def regroup_step(banks, which):
            grouped = stage.tile([P, P, QUARTERS, PACK], BF16, tag="grouped_" + which, align_bytes=64)
            words = grouped[:].bitcast(F32)
            for pair in range(2):
                regroup(banks[pair], words[:, :, 2 * pair : 2 * pair + 2, :])
            return grouped

        def quantise(pool, grouped, columns, which):
            codes = pool.tile([P, columns], U32, tag="codes_" + which, align_bytes=64)
            scales = pool.tile([P, columns], U8, tag="scales_" + which, align_bytes=64)
            nc.vector.quantize_mx(out=codes[:].bitcast(FP8X4), scales=scales[:], in_=grouped)
            return codes, scales

        def quantise_step(grouped, which):
            return quantise(stage, grouped[:].rearrange("p r j t -> p (r j t)"), B * P, which)

        def project(pool, operand, weights):
            codes, scales = operand
            w_codes, w_scales = weights
            accs = []
            for h in range(HALVES):
                acc = pool.tile([P, B, P], F32)
                w_cols = slice(h * P, (h + 1) * P)
                for b in range(B):
                    tokens = slice(b * P, (b + 1) * P)
                    nc.tensor.matmul_mx(
                        out=acc[:, b, :],
                        lhsT=codes[:, tokens].bitcast(FP8X4),
                        lhsT_scale=scales[:, tokens],
                        rhs=w_codes[:, w_cols].bitcast(FP8X4),
                        rhs_scale=w_scales[:, w_cols],
                        start=True,
                        stop=True,
                    )
                accs.append(acc)
            return accs

        def times_v_on_vector(g, v_acc, h):
            channels = slice(h * P, (h + 1) * P)
            nc.vector.tensor_tensor(
                out=ev_steps[g][:, :, channels], in0=v_acc[h][:], in1=e_steps[g][:, :, channels], op=mybir.AluOpType.mult
            )

        identity = consts.tile([P, P], F32)
        make_identity(nc, identity[:])
        warm = consts.tile([P, 1], F32)
        nc.vector.memset(warm[:], 0.0)
        nc.scalar.activation(out=warm[:], in_=warm[:], func=mybir.ActivationFunctionType.Exp)

        wk_raw = consts.tile([P, HALVES, DM], BF16)
        wv_raw = consts.tile([P, HALVES, DM], BF16)
        fetch(0, weights={"k": (wk_raw, Wk), "v": (wv_raw, Wv)})
        for c in range(1, LOAD_BUFS):
            fetch(c)

        wk_bank = transpose_weights(wk_raw)
        wk_grouped = weight_tile()
        nc.vector.tensor_copy(out=wk_grouped[:].bitcast(F32), in_=wk_bank[:].rearrange("p i u r -> p r i u"))
        wk = quantise(consts, wk_grouped[:].rearrange("p r i t -> p (r i t)"), DH, "wk")
        k_grouped = {0: regroup_step(transpose_step("k", 0), "k")}
        k_operand = quantise_step(k_grouped[0], "k")
        wv_bank = transpose_weights(wv_raw)
        wv_grouped = weight_tile()
        regroup(wv_bank, wv_grouped[:].bitcast(F32))
        v_grouped = {0: regroup_step(transpose_step("v", 0), "v")}
        k_acc = project(psum_k, k_operand, wk)
        wv = quantise(consts, wv_grouped[:].rearrange("p r i t -> p (r i t)"), DH, "wv")
        k_grouped[1] = regroup_step(transpose_step("k", 1), "k")
        v_grouped[1] = regroup_step(transpose_step("v", 1), "v")
        v_operand = None

        for g in range(STEPS):
            ahead = g + 2
            first = g == 0
            last = g == STEPS - 1
            open_results(g)

            if ahead < STEPS and not first:
                k_grouped[ahead] = regroup_step(transpose_step("k", ahead), "k")
            if not first:
                v_acc = project(psum_v, v_operand, wv)
            if ahead < STEPS and not first:
                v_banks = transpose_step("v", ahead)
                refill_after(ahead)

            tops = []
            for h in range(HALVES):
                top = maxima.tile([P, P], F32)
                nc.vector.tensor_reduce(
                    out=top[:], in_=k_acc[h][:].rearrange("p b c -> p c b"), axis=mybir.AxisListType.X, op=mybir.AluOpType.max
                )
                tops.append(top)
            if first:
                v_acc = project(psum_v, quantise_step(v_grouped[0], "v"), wv)
            for h in range(HALVES):
                e_half = e_steps[g][:, :, h * P : (h + 1) * P]
                nc.vector.tensor_tensor(
                    out=e_half, in0=k_acc[h][:], in1=tops[h][:].unsqueeze(1).to_broadcast([P, B, P]), op=mybir.AluOpType.subtract
                )
                nc.scalar.activation(out=e_half, in_=e_half, func=mybir.ActivationFunctionType.Exp)
            store(e_rows, e_pieces_of, e_pieces, g)

            if not last:
                k_acc = project(psum_k, quantise_step(k_grouped[g + 1], "k"), wk)
                if not first:
                    v_operand = quantise_step(v_grouped[g + 1], "v")

            if last:
                times_v_on_vector(g, v_acc, 0)
                times_v_on_vector(g, v_acc, 1)
            else:
                v_half = stage.tile([P, B, P], F32)
                nc.scalar.copy(out=v_half[:], in_=v_acc[1][:])
                nc.gpsimd.tensor_tensor(
                    out=ev_steps[g][:, :, P : 2 * P], in0=v_half[:], in1=e_steps[g][:, :, P : 2 * P], op=mybir.AluOpType.mult
                )
                if first:
                    k_grouped[ahead] = regroup_step(transpose_step("k", ahead), "k")
                    v_banks = transpose_step("v", ahead)
                if ahead < STEPS:
                    v_grouped[ahead] = regroup_step(v_banks, "v")
                times_v_on_vector(g, v_acc, 0)
                if first:
                    v_operand = quantise_step(v_grouped[1], "v")
            store(ev_rows, ev_pieces_of, ev_pieces, g)
